import numpy as np
import ml_dtypes


def mxq(x, axis, fmt="e4m3"):
    dtype, down = {"e4m3": (ml_dtypes.float8_e4m3fn, 7), "e5m2": (ml_dtypes.float8_e5m2, 14)}[fmt]
    v = np.moveaxis(np.asarray(x, np.float32).astype(ml_dtypes.bfloat16).astype(np.float64), axis, -1)
    blocks = v.reshape(v.shape[:-1] + (-1, 32))
    amax = np.abs(blocks).max(-1, keepdims=True)
    byte = np.maximum(np.where(amax > 0, np.frexp(amax)[1] - 1 + 127, 0) - down, 1)
    scale = np.exp2(byte - 127.0)
    codes = (blocks / scale).astype(np.float32).astype(dtype).astype(np.float64)
    return np.moveaxis((codes * scale).reshape(v.shape), -1, axis)


WIDE = False


def mx_kscale(k):
    if not WIDE:
        return np.ones(k)
    levels = np.array([10, -10, 5, -5, 0])
    if k % 512:
        return np.exp2(np.random.permutation(np.resize(levels, k // 32))).repeat(32)
    a = np.empty((k // 512, 16))
    for p in range(k // 512):
        a[p, :8] = np.random.permutation(np.resize(levels, 8))
        for g in range(8):
            far = levels[np.abs(levels - a[p, g]) >= 10]
            a[p, g + 8] = far[np.random.randint(len(far))]
    return np.exp2(a.ravel()).repeat(32)


BF16 = ml_dtypes.bfloat16


def bf(x):
    return np.asarray(x, np.float32).astype(BF16)


def f64(x):
    return np.asarray(x).astype(np.float64)


B, L, D, NC, DS = 2, 64, 512, 2, 3
EPS = 2.0 ** -23


def rmsnorm(v, w):
    ms = np.mean(np.square(v), axis=-1, keepdims=True)
    return v * (1.0 / np.sqrt(ms + EPS)) * w


def setup_inputs():
    s = mx_kscale(D)
    s = s / s.max()
    t = mx_kscale(NC * D)
    tc = t.reshape(NC, D, 1)
    return {"x": bf(np.random.standard_normal((B, L, D)) * s),
            "W_in": bf(np.random.standard_normal((NC * D, D)) / np.sqrt(D) / s[None, :]),
            "W_out": bf(np.random.standard_normal((D, NC * D)) / np.sqrt(NC * D) / t[None, :]),
            "A_theta": bf(np.random.standard_normal((NC, D, DS)) * 0.5),
            "B_real": bf(np.random.standard_normal((NC, D, DS))),
            "B_imag": bf(np.random.standard_normal((NC, D, DS))),
            "C_real": bf(np.random.standard_normal((NC, D, DS)) / np.sqrt(2 * DS) * tc),
            "C_imag": bf(np.random.standard_normal((NC, D, DS)) / np.sqrt(2 * DS) * tc),
            "norm_w": bf(1.0 + 0.1 * np.random.standard_normal(D))}


def reference(x, W_in, W_out, A_theta, B_real, B_imag, C_real, C_imag, norm_w):
    x = f64(x)
    b, l, _ = x.shape
    xi = (mxq(x, 2, "e4m3") @ mxq(f64(W_in), 1, "e4m3").T).reshape(b, l, NC, D)[..., None]
    ct = np.cos(f64(A_theta))
    st = np.sin(f64(A_theta))
    rs = np.zeros((b, l, NC, D, DS))
    is_ = np.zeros_like(rs)
    bxr = f64(B_real) * xi
    bxi = f64(B_imag) * xi
    nr = ct * rs - st * is_ + bxr
    ni = st * rs + ct * is_ + bxi
    y = np.sum(f64(C_real) * nr - f64(C_imag) * ni, axis=-1)
    out = mxq(y.reshape(b, l, NC * D), 2, "e4m3") @ mxq(f64(W_out), 1, "e4m3").T
    return x + rmsnorm(out, f64(norm_w)), nr, ni

@@ -1,0 +1,368 @@
+from contextlib import ExitStack
+
+from concourse import mybir
+from concourse.masks import make_identity
+
+F32 = mybir.dt.float32
+BF16 = mybir.dt.bfloat16
+U32 = mybir.dt.uint32
+U8 = mybir.dt.uint8
+FP8X4 = mybir.dt.float8_e4m3fn_x4
+ALU = mybir.AluOpType
+ACT = mybir.ActivationFunctionType
+
+P = 128
+D = 512
+PASSES = 2
+STATES = 3
+COLS = PASSES * D
+HALF = 256
+SLICE_FLAT = HALF * STATES
+SLICE_WORDS = SLICE_FLAT // 2
+SLICES = COLS // HALF
+FLAT = SLICES * SLICE_FLAT
+BANK = 512
+NORM_ROW = 2 * SLICES
+EPS = 2.0 ** -23
+
+FLOPS = 2 * (2 * P * D * COLS)
+
+
+def tile_mamba3core_s_kernel(
+    tc, x, W_in, W_out, A_theta, B_real, B_imag, C_real, C_imag, norm_w, out_0, out_1, out_2
+):
+    nc = tc.nc
+    x_rows = x.flatten_outer_dims()
+    res_rows = out_0.flatten_outer_dims()
+    state_rows = {
+        "r": out_1.rearrange("b l c d n -> (b l) (c d n)"),
+        "i": out_2.rearrange("b l c d n -> (b l) (c d n)"),
+    }
+
+    with ExitStack() as ctx:
+        keep = ctx.enter_context(tc.tile_pool(name="keep", bufs=1))
+        flips = ctx.enter_context(tc.psum_pool(name="flips", bufs=3))
+        spreads = ctx.enter_context(tc.psum_pool(name="spreads", bufs=2))
+        xi_tok = ctx.enter_context(tc.psum_pool(name="xi_tok", bufs=1))
+        xi_col = ctx.enter_context(tc.psum_pool(name="xi_col", bufs=2))
+        ctx.enter_context(tc.manual_schedule())
+
+        vec_rows = keep.tile([P, SLICE_FLAT], BF16)
+        nc.gpsimd.memset(vec_rows[:].bitcast(F32), 0.0)
+        ident = keep.tile([P, P], F32)
+        make_identity(nc, ident[:])
+        eps = keep.tile([P, 1], F32)
+        nc.vector.memset(eps[:], EPS)
+
+        x_sb = keep.tile([P, D], BF16)
+        nc.sync.dma_start(out=x_sb[:], in_=x_rows)
+        wi_sb = keep.tile([P, PASSES, 2, 2 * D], BF16)
+
+        def load_w_in(h, a):
+            nc.sync.dma_start(
+                out=wi_sb[:, h, a, :],
+                in_=W_in[D * h : D * (h + 1), :].rearrange("(p a e) k -> p a (e k)", a=2, e=2)[:, a, :],
+            )
+
+        load_w_in(0, 0)
+        load_w_in(0, 1)
+        for v, src in enumerate((B_real, B_imag)):
+            nc.sync.dma_start(
+                out=vec_rows[SLICES * v : SLICES * (v + 1), :],
+                in_=src.rearrange("a d n -> (a d n)").rearrange("(g f) -> g f", f=SLICE_FLAT),
+            )
+        nc.sync.dma_start(
+            out=vec_rows[NORM_ROW : NORM_ROW + 1, 0:D], in_=norm_w.rearrange("(o d) -> o d", o=1)
+        )
+        load_w_in(1, 0)
+        own = keep.tile([P, 4, PASSES, 16], BF16)
+        for v, src in enumerate((B_real, B_imag, C_real, C_imag)):
+            nc.sync.dma_start(
+                out=own[:, v, :, 0 : 4 * STATES],
+                in_=src.rearrange("h (p t) n -> p h (t n)", t=4),
+            )
+        load_w_in(1, 1)
+        wo_sb = keep.tile([P, 4, COLS], BF16)
+        for pair in range(2):
+            nc.sync.dma_start(
+                out=wo_sb[:, 2 * pair : 2 * pair + 2, :],
+                in_=W_out[256 * pair : 256 * (pair + 1), :].rearrange("(i q) k -> q i k", q=P),
+            )
+        warm = keep.tile([P, 1], F32)
+        nc.scalar.activation(out=warm[:], in_=eps[:], func=ACT.Sqrt)
+
+        vec_words = vec_rows[:].bitcast(F32)
+        vec_cols = keep.tile([P, 3, 16], F32)
+        rr = keep.tile([P, PASSES, 4 * STATES], F32)
+        ii = keep.tile([P, PASSES, 4 * STATES], F32)
+        gain = keep.tile([P, PASSES, 4], F32)
+
+        def turn_for_spreading():
+            bank = flips.tile([P, BANK], F32, tag="flip")
+            for s in range(3):
+                nc.tensor.transpose(
+                    bank[:, P * s : P * (s + 1)], vec_words[:, P * s : P * (s + 1)], ident[:]
+                )
+            nc.scalar.copy(
+                out=vec_cols[:], in_=bank[:, 0 : 3 * P].rearrange("w (s r) -> w s r", s=3)[:, :, 0:16]
+            )
+
+        def make_gain():
+            used = slice(0, 4 * STATES)
+            nc.vector.tensor_tensor(out=rr[:], in0=own[:, 2, :, used], in1=own[:, 0, :, used], op=ALU.mult)
+            nc.vector.tensor_tensor(out=ii[:], in0=own[:, 3, :, used], in1=own[:, 1, :, used], op=ALU.mult)
+            nc.vector.tensor_tensor(out=rr[:], in0=rr[:], in1=ii[:], op=ALU.subtract)
+            nc.vector.tensor_reduce(
+                out=gain[:].rearrange("p h t -> p (h t)"),
+                in_=rr[:].rearrange("p h (t n) -> p (h t) n", n=STATES),
+                axis=mybir.AxisListType.X,
+                op=ALU.add,
+            )
+
+        def spread_row(pool, row, slices):
+            bank = pool.tile([P, BANK], F32, tag="flip")
+            for s in range(slices):
+                nc.tensor.transpose(
+                    bank[:, P * s : P * (s + 1)],
+                    vec_cols[:, s, row : row + 1].to_broadcast([P, P]),
+                    ident[:],
+                )
+            return bank
+
+        b_imag_all = keep.tile([P, FLAT], BF16)
+        norm_w_all = keep.tile([P, D], BF16)
+
+        def spread_b_imag(g):
+            bank = spread_row(flips, SLICES + g, 3)
+            nc.scalar.copy(
+                out=b_imag_all[:].bitcast(F32)[:, SLICE_WORDS * g : SLICE_WORDS * (g + 1)],
+                in_=bank[:, 0:SLICE_WORDS],
+            )
+
+        def spread_norm_w():
+            bank = spread_row(flips, NORM_ROW, 2)
+            nc.scalar.copy(out=norm_w_all[:].bitcast(F32), in_=bank[:, 0 : D // 2])
+
+        x_grouped = keep.tile([P, P * 4], BF16, align_bytes=64)
+        x_codes = keep.tile([P, P], U32, align_bytes=64)
+        x_scales = keep.tile([P, P], U8, align_bytes=64)
+
+        def flip_x():
+            bank = flips.tile([P, BANK], F32, tag="flip")
+            for u in range(2):
+                nc.tensor.transpose(
+                    bank[:, P * u : P * (u + 1)], x_sb[:].bitcast(F32)[:, u : 2 * P : 2], ident[:]
+                )
+            nc.vector.tensor_copy(
+                out=x_grouped[:].bitcast(F32).rearrange("w (t u) -> w t u", u=2),
+                in_=bank[:, 0 : 2 * P].rearrange("w (u t) -> w t u", u=2),
+            )
+            nc.vector.quantize_mx(out=x_codes[:].bitcast(FP8X4), scales=x_scales[:], in_=x_grouped[:])
+
+        wi_grouped = keep.tile([P, COLS * 4], BF16, align_bytes=64)
+        wi_codes = keep.tile([P, COLS], U32, align_bytes=64)
+        wi_scales = keep.tile([P, COLS], U8, align_bytes=64)
+
+        def flip_w_in(h, a, copy):
+            bank = flips.tile([P, BANK], F32, tag="flip")
+            for e in range(2):
+                for u in range(2):
+                    nc.tensor.transpose(
+                        bank[:, P * (2 * e + u) : P * (2 * e + u + 1)],
+                        wi_sb[:, h, a, :].bitcast(F32)[:, 256 * e + u : 256 * (e + 1) : 2],
+                        ident[:],
+                    )
+            first = BANK * (2 * h + a)
+            copy(
+                out=wi_grouped[:].bitcast(F32)[:, first : first + BANK].rearrange(
+                    "w (e p u) -> w e p u", e=2, u=2
+                ),
+                in_=bank[:].rearrange("w (e u p) -> w e p u", e=2, u=2),
+            )
+
+        def quantise_w_in(h, a):
+            first = D * h + HALF * a
+            nc.vector.quantize_mx(
+                out=wi_codes[:, first : first + HALF].bitcast(FP8X4),
+                scales=wi_scales[:, first : first + HALF],
+                in_=wi_grouped[:, 4 * first : 4 * (first + HALF)],
+            )
+
+        state_sb = {
+            "r": keep.tile([P, FLAT], F32, name="state_r"),
+            "i": keep.tile([P, FLAT], F32, name="state_i"),
+        }
+        xi_sb = keep.tile([P, COLS], F32)
+        y_grouped = keep.tile([P, PASSES, P, 4], BF16, align_bytes=64)
+        y_codes = keep.tile([P, PASSES, P], U32, align_bytes=64)
+        y_scales = keep.tile([P, PASSES, P], U8, align_bytes=64)
+        xi_by_token = {}
+        xi_by_column = {}
+
+        def first_matmul(h, a):
+            if a == 0:
+                xi_by_token[h] = xi_tok.tile([P, D], F32, name="xi_by_token", tag="xi_tok")
+                xi_by_column[h] = xi_col.tile([P, 4, P], F32, name="xi_by_column", tag="xi_col")
+            cols = slice(D * h + HALF * a, D * h + HALF * (a + 1))
+            nc.tensor.matmul_mx(
+                out=xi_by_token[h][:, HALF * a : HALF * (a + 1)],
+                lhsT=x_codes[:].bitcast(FP8X4),
+                lhsT_scale=x_scales[:],
+                rhs=wi_codes[:, cols].bitcast(FP8X4),
+                rhs_scale=wi_scales[:, cols],
+                start=True,
+                stop=True,
+            )
+            for t in (2 * a, 2 * a + 1):
+                part = slice(D * h + P * t, D * h + P * (t + 1))
+                nc.tensor.matmul_mx(
+                    out=xi_by_column[h][:, t, :],
+                    lhsT=wi_codes[:, part].bitcast(FP8X4),
+                    lhsT_scale=wi_scales[:, part],
+                    rhs=x_codes[:].bitcast(FP8X4),
+                    rhs_scale=x_scales[:],
+                    start=True,
+                    stop=True,
+                )
+
+        def copy_xi(g):
+            h, half = divmod(g, 2)
+            nc.scalar.copy(
+                out=xi_sb[:, HALF * g : HALF * (g + 1)].rearrange("x (p t) -> x p t", t=4),
+                in_=xi_by_token[h][:].rearrange("x (t p) -> x p t", t=4)[:, 64 * half : 64 * (half + 1), :],
+            )
+
+        def states(which, g, engine, b_all):
+            flat = slice(SLICE_FLAT * g, SLICE_FLAT * (g + 1))
+            cols = slice(HALF * g, HALF * (g + 1))
+            engine.tensor_tensor(
+                out=state_sb[which][:, flat].rearrange("t (c n) -> t c n", n=STATES),
+                in0=xi_sb[:, cols].unsqueeze(2).to_broadcast([P, HALF, STATES]),
+                in1=b_all.rearrange("t (c n) -> t c n", n=STATES),
+                op=ALU.mult,
+            )
+            nc.sync.dma_start(out=state_rows[which][:, flat], in_=state_sb[which][:, flat])
+
+        def states_imag(g):
+            states("i", g, nc.gpsimd, b_imag_all[:, SLICE_FLAT * g : SLICE_FLAT * (g + 1)])
+
+        def states_real(g):
+            bank = spread_row(spreads, g, 3)
+            states("r", g, nc.vector, bank[:, 0:SLICE_WORDS].bitcast(BF16))
+
+        def make_y(h):
+            nc.vector.tensor_tensor(
+                out=y_grouped[:, h, :, :],
+                in0=xi_by_column[h][:].rearrange("p j t -> p t j"),
+                in1=gain[:, h, :].unsqueeze(1).to_broadcast([P, P, 4]),
+                op=ALU.mult,
+            )
+
+        def quantise_y(h):
+            nc.vector.quantize_mx(
+                out=y_codes[:, h, :].bitcast(FP8X4),
+                scales=y_scales[:, h, :],
+                in_=y_grouped[:, h, :, :].rearrange("p t j -> p (t j)"),
+            )
+
+        wo_grouped = keep.tile([P, PASSES, D * 4], BF16, align_bytes=64)
+        wo_codes = keep.tile([P, PASSES, D], U32, align_bytes=64)
+        wo_scales = keep.tile([P, PASSES, D], U8, align_bytes=64)
+
+        def flip_w_out(pair, h):
+            bank = flips.tile([P, BANK], F32, tag="flip")
+            for il in range(2):
+                for u in range(2):
+                    nc.tensor.transpose(
+                        bank[:, P * (2 * il + u) : P * (2 * il + u + 1)],
+                        wo_sb[:, 2 * pair + il, :].bitcast(F32)[:, 256 * h + u : 256 * (h + 1) : 2],
+                        ident[:],
+                    )
+            nc.scalar.copy(
+                out=wo_grouped[:, h, :].bitcast(F32)[:, BANK * pair : BANK * (pair + 1)].rearrange(
+                    "p (il q u) -> p il q u", il=2, u=2
+                ),
+                in_=bank[:].rearrange("p (il u q) -> p il q u", il=2, u=2),
+            )
+
+        def quantise_w_out(pair, h):
+            rows = slice(256 * pair, 256 * (pair + 1))
+            nc.vector.quantize_mx(
+                out=wo_codes[:, h, rows].bitcast(FP8X4),
+                scales=wo_scales[:, h, rows],
+                in_=wo_grouped[:, h, 4 * 256 * pair : 4 * 256 * (pair + 1)],
+            )
+
+        flip_x()
+        flip_w_in(0, 0, nc.scalar.copy)
+        flip_w_in(0, 1, nc.vector.tensor_copy)
+        turn_for_spreading()
+        quantise_w_in(0, 0)
+        quantise_w_in(0, 1)
+        spread_b_imag(0)
+
+        first_matmul(0, 0)
+        first_matmul(0, 1)
+        copy_xi(0)
+        states_imag(0)
+        states_real(0)
+        flip_w_in(1, 0, nc.scalar.copy)
+        copy_xi(1)
+        spread_b_imag(1)
+        make_gain()
+        states_imag(1)
+        states_real(1)
+        flip_w_in(1, 1, nc.scalar.copy)
+        quantise_w_in(1, 0)
+        make_y(0)
+        quantise_w_in(1, 1)
+        quantise_y(0)
+        spread_b_imag(2)
+
+        first_matmul(1, 0)
+        first_matmul(1, 1)
+        copy_xi(2)
+        states_imag(2)
+        make_y(1)
+        states_real(2)
+        quantise_y(1)
+        flip_w_out(0, 0)
+        flip_w_out(0, 1)
+        copy_xi(3)
+        spread_b_imag(3)
+        states_imag(3)
+        flip_w_out(1, 0)
+        flip_w_out(1, 1)
+        quantise_w_out(0, 0)
+        quantise_w_out(0, 1)
+        quantise_w_out(1, 0)
+        quantise_w_out(1, 1)
+        states_real(3)
+        spread_norm_w()
+
+        acc = xi_col.tile([P, D], F32, tag="xi_col")
+        for h in range(PASSES):
+            nc.tensor.matmul_mx(
+                out=acc[:],
+                lhsT=y_codes[:, h, :].bitcast(FP8X4),
+                lhsT_scale=y_scales[:, h, :],
+                rhs=wo_codes[:, h, :].bitcast(FP8X4),
+                rhs_scale=wo_scales[:, h, :],
+                start=(h == 0),
+                stop=(h == PASSES - 1),
+            )
+
+        squares = keep.tile([P, D], F32)
+        sum_sq = keep.tile([P, 1], F32)
+        nc.scalar.activation(out=squares[:], in_=acc[:], func=ACT.Square, accum_out=sum_sq[:])
+        rms = keep.tile([P, 1], F32)
+        nc.scalar.activation(out=rms[:], in_=sum_sq[:], func=ACT.Sqrt, bias=eps[:], scale=1.0 / D)
+        weighted = keep.tile([P, D], F32)
+        nc.vector.tensor_tensor(out=weighted[:], in0=acc[:], in1=norm_w_all[:], op=ALU.mult)
+        inv_rms = keep.tile([P, 1], F32)
+        nc.vector.reciprocal(out=inv_rms[:], in_=rms[:])
+        res = keep.tile([P, D], F32)
+        nc.vector.scalar_tensor_tensor(
+            out=res[:], in0=weighted[:], scalar=inv_rms[:], in1=x_sb[:], op0=ALU.mult, op1=ALU.add
+        )
+        nc.sync.dma_start(out=res_rows, in_=res[:])

@@ -48,7 +48,7 @@ def tile_mamba3core_s_kernel(
         ctx.enter_context(tc.manual_schedule())
 
         vec_rows = keep.tile([P, SLICE_FLAT], BF16)
-        nc.gpsimd.memset(vec_rows[:].bitcast(F32), 0.0)
+        nc.vector.memset(vec_rows[:].bitcast(F32), 0.0)
         ident = keep.tile([P, P], F32)
         make_identity(nc, ident[:])
         eps = keep.tile([P, 1], F32)
@@ -56,16 +56,15 @@ def tile_mamba3core_s_kernel(
 
         x_sb = keep.tile([P, D], BF16)
         nc.sync.dma_start(out=x_sb[:], in_=x_rows)
-        wi_sb = keep.tile([P, PASSES, 2, 2 * D], BF16)
+        wi_sb = keep.tile([P, SLICES, 2 * D], BF16)
 
-        def load_w_in(h, a):
+        def load_w_in(g):
             nc.sync.dma_start(
-                out=wi_sb[:, h, a, :],
-                in_=W_in[D * h : D * (h + 1), :].rearrange("(p a e) k -> p a (e k)", a=2, e=2)[:, a, :],
+                out=wi_sb[:, g, :],
+                in_=W_in[HALF * g : HALF * (g + 1), :].rearrange("(q e) k -> q (e k)", e=2),
             )
 
-        load_w_in(0, 0)
-        load_w_in(0, 1)
+        load_w_in(0)
         for v, src in enumerate((B_real, B_imag)):
             nc.sync.dma_start(
                 out=vec_rows[SLICES * v : SLICES * (v + 1), :],
@@ -74,14 +73,15 @@ def tile_mamba3core_s_kernel(
         nc.sync.dma_start(
             out=vec_rows[NORM_ROW : NORM_ROW + 1, 0:D], in_=norm_w.rearrange("(o d) -> o d", o=1)
         )
-        load_w_in(1, 0)
+        load_w_in(1)
         own = keep.tile([P, 4, PASSES, 16], BF16)
         for v, src in enumerate((B_real, B_imag, C_real, C_imag)):
             nc.sync.dma_start(
                 out=own[:, v, :, 0 : 4 * STATES],
                 in_=src.rearrange("h (p t) n -> p h (t n)", t=4),
             )
-        load_w_in(1, 1)
+        load_w_in(2)
+        load_w_in(3)
         wo_sb = keep.tile([P, 4, COLS], BF16)
         for pair in range(2):
             nc.sync.dma_start(
@@ -89,7 +89,7 @@ def tile_mamba3core_s_kernel(
                 in_=W_out[256 * pair : 256 * (pair + 1), :].rearrange("(i q) k -> q i k", q=P),
             )
         warm = keep.tile([P, 1], F32)
-        nc.scalar.activation(out=warm[:], in_=eps[:], func=ACT.Sqrt)
+        nc.scalar.activation(out=warm[:], in_=eps[:], func=ACT.Abs_reciprocal_sqrt)
 
         vec_words = vec_rows[:].bitcast(F32)
         vec_cols = keep.tile([P, 3, 16], F32)
@@ -109,15 +109,13 @@ def tile_mamba3core_s_kernel(
 
         def make_gain():
             used = slice(0, 4 * STATES)
-            nc.vector.tensor_tensor(out=rr[:], in0=own[:, 2, :, used], in1=own[:, 0, :, used], op=ALU.mult)
-            nc.vector.tensor_tensor(out=ii[:], in0=own[:, 3, :, used], in1=own[:, 1, :, used], op=ALU.mult)
-            nc.vector.tensor_tensor(out=rr[:], in0=rr[:], in1=ii[:], op=ALU.subtract)
-            nc.vector.tensor_reduce(
-                out=gain[:].rearrange("p h t -> p (h t)"),
-                in_=rr[:].rearrange("p h (t n) -> p (h t) n", n=STATES),
-                axis=mybir.AxisListType.X,
-                op=ALU.add,
-            )
+            nc.gpsimd.tensor_tensor(out=rr[:], in0=own[:, 2, :, used], in1=own[:, 0, :, used], op=ALU.mult)
+            nc.gpsimd.tensor_tensor(out=ii[:], in0=own[:, 3, :, used], in1=own[:, 1, :, used], op=ALU.mult)
+            nc.gpsimd.tensor_tensor(out=rr[:], in0=rr[:], in1=ii[:], op=ALU.subtract)
+            terms = rr[:].rearrange("p h (t n) -> p (h t) n", n=STATES)
+            total = gain[:].rearrange("p h t -> p (h t)")
+            nc.gpsimd.tensor_tensor(out=total, in0=terms[:, :, 0], in1=terms[:, :, 1], op=ALU.add)
+            nc.gpsimd.tensor_tensor(out=total, in0=total, in1=terms[:, :, 2], op=ALU.add)
 
         def spread_row(pool, row, slices):
             bank = pool.tile([P, BANK], F32, tag="flip")
@@ -162,30 +160,40 @@ def tile_mamba3core_s_kernel(
         wi_grouped = keep.tile([P, COLS * 4], BF16, align_bytes=64)
         wi_codes = keep.tile([P, COLS], U32, align_bytes=64)
         wi_scales = keep.tile([P, COLS], U8, align_bytes=64)
+        wi_words = wi_grouped[:].bitcast(F32).rearrange("w (h r e p u) -> w h r e p u", h=2, r=2, e=2, u=2)
 
-        def flip_w_in(h, a, copy):
-            bank = flips.tile([P, BANK], F32, tag="flip")
+        def flip_w_in(g, copies):
+            h, half = divmod(g, 2)
+            banks = [flips.tile([P, BANK], F32, name="bank", tag="flip")]
+            banks.append(banks[0] if copies[0] == copies[1] else flips.tile([P, BANK], F32, name="bank", tag="flip"))
             for e in range(2):
                 for u in range(2):
                     nc.tensor.transpose(
-                        bank[:, P * (2 * e + u) : P * (2 * e + u + 1)],
-                        wi_sb[:, h, a, :].bitcast(F32)[:, 256 * e + u : 256 * (e + 1) : 2],
+                        banks[e][:, P * (2 * e + u) : P * (2 * e + u + 1)],
+                        wi_sb[:, g, :].bitcast(F32)[:, 256 * e + u : 256 * (e + 1) : 2],
                         ident[:],
                     )
-            first = BANK * (2 * h + a)
-            copy(
-                out=wi_grouped[:].bitcast(F32)[:, first : first + BANK].rearrange(
-                    "w (e p u) -> w e p u", e=2, u=2
-                ),
-                in_=bank[:].rearrange("w (e u p) -> w e p u", e=2, u=2),
-            )
+            for e in range(2):
+                copies[e](
+                    out=wi_words[:, h, :, e, 64 * half : 64 * (half + 1), :],
+                    in_=banks[e][:, HALF * e : HALF * (e + 1)].rearrange("w (u p r) -> w r p u", u=2, r=2),
+                )
 
-        def quantise_w_in(h, a):
-            first = D * h + HALF * a
+        def quantise_w_in_slice(g):
+            h, half = divmod(g, 2)
+            for t in range(4):
+                first = D * h + P * t + 64 * half
+                nc.vector.quantize_mx(
+                    out=wi_codes[:, first : first + 64].bitcast(FP8X4),
+                    scales=wi_scales[:, first : first + 64],
+                    in_=wi_grouped[:, 4 * first : 4 * (first + 64)],
+                )
+
+        def quantise_w_in(h):
             nc.vector.quantize_mx(
-                out=wi_codes[:, first : first + HALF].bitcast(FP8X4),
-                scales=wi_scales[:, first : first + HALF],
-                in_=wi_grouped[:, 4 * first : 4 * (first + HALF)],
+                out=wi_codes[:, D * h : D * (h + 1)].bitcast(FP8X4),
+                scales=wi_scales[:, D * h : D * (h + 1)],
+                in_=wi_grouped[:, 4 * D * h : 4 * D * (h + 1)],
             )
 
         state_sb = {
@@ -199,13 +207,9 @@ def tile_mamba3core_s_kernel(
         xi_by_token = {}
         xi_by_column = {}
 
-        def first_matmul(h, a):
-            if a == 0:
-                xi_by_token[h] = xi_tok.tile([P, D], F32, name="xi_by_token", tag="xi_tok")
-                xi_by_column[h] = xi_col.tile([P, 4, P], F32, name="xi_by_column", tag="xi_col")
-            cols = slice(D * h + HALF * a, D * h + HALF * (a + 1))
+        def token_pass(out, cols):
             nc.tensor.matmul_mx(
-                out=xi_by_token[h][:, HALF * a : HALF * (a + 1)],
+                out=out,
                 lhsT=x_codes[:].bitcast(FP8X4),
                 lhsT_scale=x_scales[:],
                 rhs=wi_codes[:, cols].bitcast(FP8X4),
@@ -213,7 +217,26 @@ def tile_mamba3core_s_kernel(
                 start=True,
                 stop=True,
             )
-            for t in (2 * a, 2 * a + 1):
+
+        def token_matmul_slice(g):
+            h, half = divmod(g, 2)
+            bank = xi_tok.tile([P, D], F32, name="xi_by_token", tag="xi_tok")
+            for t in range(4):
+                first = D * h + P * t + 64 * half
+                token_pass(bank[:, 64 * t : 64 * (t + 1)], slice(first, first + 64))
+            xi_by_token[g] = bank[:, 0:HALF].rearrange("x (t p) -> x p t", t=4)
+
+        def token_matmul(h):
+            bank = xi_tok.tile([P, D], F32, name="xi_by_token", tag="xi_tok")
+            token_pass(bank[:], slice(D * h, D * (h + 1)))
+            for half in range(2):
+                xi_by_token[2 * h + half] = bank[:].rearrange("x (t p) -> x p t", t=4)[
+                    :, 64 * half : 64 * (half + 1), :
+                ]
+
+        def column_matmul(h):
+            xi_by_column[h] = xi_col.tile([P, 4, P], F32, name="xi_by_column", tag="xi_col")
+            for t in range(4):
                 part = slice(D * h + P * t, D * h + P * (t + 1))
                 nc.tensor.matmul_mx(
                     out=xi_by_column[h][:, t, :],
@@ -226,10 +249,9 @@ def tile_mamba3core_s_kernel(
                 )
 
         def copy_xi(g):
-            h, half = divmod(g, 2)
             nc.scalar.copy(
                 out=xi_sb[:, HALF * g : HALF * (g + 1)].rearrange("x (p t) -> x p t", t=4),
-                in_=xi_by_token[h][:].rearrange("x (t p) -> x p t", t=4)[:, 64 * half : 64 * (half + 1), :],
+                in_=xi_by_token[g],
             )
 
         def states(which, g, engine, b_all):
@@ -241,14 +263,16 @@ def tile_mamba3core_s_kernel(
                 in1=b_all.rearrange("t (c n) -> t c n", n=STATES),
                 op=ALU.mult,
             )
+
+        def store(which, g):
+            flat = slice(SLICE_FLAT * g, SLICE_FLAT * (g + 1))
             nc.sync.dma_start(out=state_rows[which][:, flat], in_=state_sb[which][:, flat])
 
-        def states_imag(g):
-            states("i", g, nc.gpsimd, b_imag_all[:, SLICE_FLAT * g : SLICE_FLAT * (g + 1)])
+        def states_gpsimd(which, g):
+            states(which, g, nc.gpsimd, b_imag_all[:, SLICE_FLAT * g : SLICE_FLAT * (g + 1)])
 
-        def states_real(g):
-            bank = spread_row(spreads, g, 3)
-            states("r", g, nc.vector, bank[:, 0:SLICE_WORDS].bitcast(BF16))
+        def states_vector(which, g, bank):
+            states(which, g, nc.vector, bank[:, 0:SLICE_WORDS].bitcast(BF16))
 
         def make_y(h):
             nc.vector.tensor_tensor(
@@ -293,74 +317,103 @@ def tile_mamba3core_s_kernel(
                 in_=wo_grouped[:, h, 4 * 256 * pair : 4 * 256 * (pair + 1)],
             )
 
-        flip_x()
-        flip_w_in(0, 0, nc.scalar.copy)
-        flip_w_in(0, 1, nc.vector.tensor_copy)
-        turn_for_spreading()
-        quantise_w_in(0, 0)
-        quantise_w_in(0, 1)
-        spread_b_imag(0)
-
-        first_matmul(0, 0)
-        first_matmul(0, 1)
-        copy_xi(0)
-        states_imag(0)
-        states_real(0)
-        flip_w_in(1, 0, nc.scalar.copy)
-        copy_xi(1)
-        spread_b_imag(1)
         make_gain()
-        states_imag(1)
-        states_real(1)
-        flip_w_in(1, 1, nc.scalar.copy)
-        quantise_w_in(1, 0)
-        make_y(0)
-        quantise_w_in(1, 1)
-        quantise_y(0)
-        spread_b_imag(2)
-
-        first_matmul(1, 0)
-        first_matmul(1, 1)
-        copy_xi(2)
-        states_imag(2)
-        make_y(1)
-        states_real(2)
-        quantise_y(1)
+        flip_x()
+        flip_w_in(0, (nc.vector.tensor_copy, nc.scalar.copy))
+        turn_for_spreading()
+        quantise_w_in_slice(0)
+        flip_w_in(1, (nc.vector.tensor_copy, nc.scalar.copy))
+        token_matmul_slice(0)
+        copy_xi(0)
+        spread_b_imag(0)
+        b_real_0 = spread_row(spreads, 0, 3)
+        quantise_w_in_slice(1)
+        states_vector("r", 0, b_real_0)
+        store("r", 0)
+        states_gpsimd("i", 0)
+        token_matmul_slice(1)
+        b_real_1 = spread_row(spreads, 1, 3)
+        copy_xi(1)
+        states_vector("r", 1, b_real_1)
+        store("r", 1)
+        flip_w_in(2, (nc.scalar.copy, nc.scalar.copy))
+        flip_w_in(3, (nc.vector.tensor_copy, nc.vector.tensor_copy))
+        store("i", 0)
+        quantise_w_in(1)
+        column_matmul(0)
+        b_imag_1 = spread_row(spreads, 5, 3)
+        states_vector("i", 1, b_imag_1)
+        store("i", 1)
         flip_w_out(0, 0)
-        flip_w_out(0, 1)
-        copy_xi(3)
-        spread_b_imag(3)
-        states_imag(3)
         flip_w_out(1, 0)
-        flip_w_out(1, 1)
+        make_y(0)
+        token_matmul(1)
+        copy_xi(2)
+        column_matmul(1)
         quantise_w_out(0, 0)
-        quantise_w_out(0, 1)
         quantise_w_out(1, 0)
+        spread_b_imag(2)
+        states_gpsimd("i", 2)
+        b_real_2 = spread_row(spreads, 2, 3)
+        make_y(1)
+        states_vector("r", 2, b_real_2)
+        store("r", 2)
+        flip_w_out(0, 1)
+        flip_w_out(1, 1)
+        copy_xi(3)
+        quantise_y(0)
+        quantise_y(1)
+        quantise_w_out(0, 1)
         quantise_w_out(1, 1)
-        states_real(3)
+        spread_b_imag(3)
+        states_gpsimd("i", 3)
+        b_real_3 = spread_row(spreads, 3, 3)
         spread_norm_w()
+        states_vector("r", 3, b_real_3)
+        store("r", 3)
+        store("i", 2)
+        store("i", 3)
 
-        acc = xi_col.tile([P, D], F32, tag="xi_col")
-        for h in range(PASSES):
-            nc.tensor.matmul_mx(
-                out=acc[:],
-                lhsT=y_codes[:, h, :].bitcast(FP8X4),
-                lhsT_scale=y_scales[:, h, :],
-                rhs=wo_codes[:, h, :].bitcast(FP8X4),
-                rhs_scale=wo_scales[:, h, :],
-                start=(h == 0),
-                stop=(h == PASSES - 1),
-            )
+        acc = [xi_col.tile([P, HALF], F32, name="acc", tag="xi_col") for n in range(2)]
+        for n in range(2):
+            cols = slice(HALF * n, HALF * (n + 1))
+            for h in range(PASSES):
+                nc.tensor.matmul_mx(
+                    out=acc[n][:],
+                    lhsT=y_codes[:, h, :].bitcast(FP8X4),
+                    lhsT_scale=y_scales[:, h, :],
+                    rhs=wo_codes[:, h, cols].bitcast(FP8X4),
+                    rhs_scale=wo_scales[:, h, cols],
+                    start=(h == 0),
+                    stop=(h == PASSES - 1),
+                )
 
         squares = keep.tile([P, D], F32)
-        sum_sq = keep.tile([P, 1], F32)
-        nc.scalar.activation(out=squares[:], in_=acc[:], func=ACT.Square, accum_out=sum_sq[:])
-        rms = keep.tile([P, 1], F32)
-        nc.scalar.activation(out=rms[:], in_=sum_sq[:], func=ACT.Sqrt, bias=eps[:], scale=1.0 / D)
+        sum_sq = keep.tile([P, 2], F32)
         weighted = keep.tile([P, D], F32)
-        nc.vector.tensor_tensor(out=weighted[:], in0=acc[:], in1=norm_w_all[:], op=ALU.mult)
+        mean_sq = keep.tile([P, 1], F32)
         inv_rms = keep.tile([P, 1], F32)
-        nc.vector.reciprocal(out=inv_rms[:], in_=rms[:])
+
+        def square_half(n):
+            nc.scalar.activation(
+                out=squares[:, HALF * n : HALF * (n + 1)],
+                in_=acc[n][:],
+                func=ACT.Square,
+                accum_out=sum_sq[:, n : n + 1],
+            )
+
+        def weigh_half(n):
+            cols = slice(HALF * n, HALF * (n + 1))
+            nc.vector.tensor_tensor(out=weighted[:, cols], in0=acc[n][:], in1=norm_w_all[:, cols], op=ALU.mult)
+
+        square_half(0)
+        weigh_half(1)
+        nc.scalar.activation(out=mean_sq[:], in_=sum_sq[:, 0:1], func=ACT.Identity, bias=eps[:], scale=1.0 / D)
+        square_half(1)
+        weigh_half(0)
+        nc.scalar.activation(
+            out=inv_rms[:], in_=sum_sq[:, 1:2], func=ACT.Abs_reciprocal_sqrt, bias=mean_sq[:], scale=1.0 / D
+        )
         res = keep.tile([P, D], F32)
         nc.vector.scalar_tensor_tensor(
             out=res[:], in0=weighted[:], scalar=inv_rms[:], in1=x_sb[:], op0=ALU.mult, op1=ALU.add

@@ -74,12 +74,6 @@ def tile_mamba3core_s_kernel(
             out=vec_rows[NORM_ROW : NORM_ROW + 1, 0:D], in_=norm_w.rearrange("(o d) -> o d", o=1)
         )
         load_w_in(1)
-        own = keep.tile([P, 4, PASSES, 16], BF16)
-        for v, src in enumerate((B_real, B_imag, C_real, C_imag)):
-            nc.sync.dma_start(
-                out=own[:, v, :, 0 : 4 * STATES],
-                in_=src.rearrange("h (p t) n -> p h (t n)", t=4),
-            )
         load_w_in(2)
         load_w_in(3)
         wo_sb = keep.tile([P, 4, COLS], BF16)
@@ -87,6 +81,12 @@ def tile_mamba3core_s_kernel(
             nc.sync.dma_start(
                 out=wo_sb[:, 2 * pair : 2 * pair + 2, :],
                 in_=W_out[256 * pair : 256 * (pair + 1), :].rearrange("(i q) k -> q i k", q=P),
+            )
+        own = keep.tile([P, 4, PASSES, 16], BF16)
+        for v, src in enumerate((B_real, B_imag, C_real, C_imag)):
+            nc.sync.dma_start(
+                out=own[:, v, :, 0 : 4 * STATES],
+                in_=src.rearrange("h (p t) n -> p h (t n)", t=4),
             )
         warm = keep.tile([P, 1], F32)
         nc.scalar.activation(out=warm[:], in_=eps[:], func=ACT.Abs_reciprocal_sqrt)
@@ -282,18 +282,18 @@ def tile_mamba3core_s_kernel(
                 op=ALU.mult,
             )
 
-        def quantise_y(h):
+        def quantise_y():
             nc.vector.quantize_mx(
-                out=y_codes[:, h, :].bitcast(FP8X4),
-                scales=y_scales[:, h, :],
-                in_=y_grouped[:, h, :, :].rearrange("p t j -> p (t j)"),
+                out=y_codes[:].rearrange("p h t -> p (h t)").bitcast(FP8X4),
+                scales=y_scales[:].rearrange("p h t -> p (h t)"),
+                in_=y_grouped[:].rearrange("p h t j -> p (h t j)"),
             )
 
         wo_grouped = keep.tile([P, PASSES, D * 4], BF16, align_bytes=64)
         wo_codes = keep.tile([P, PASSES, D], U32, align_bytes=64)
         wo_scales = keep.tile([P, PASSES, D], U8, align_bytes=64)
 
-        def flip_w_out(pair, h):
+        def flip_w_out(pair, h, copy):
             bank = flips.tile([P, BANK], F32, tag="flip")
             for il in range(2):
                 for u in range(2):
@@ -302,22 +302,18 @@ def tile_mamba3core_s_kernel(
                         wo_sb[:, 2 * pair + il, :].bitcast(F32)[:, 256 * h + u : 256 * (h + 1) : 2],
                         ident[:],
                     )
-            nc.scalar.copy(
+            copy(
                 out=wo_grouped[:, h, :].bitcast(F32)[:, BANK * pair : BANK * (pair + 1)].rearrange(
                     "p (il q u) -> p il q u", il=2, u=2
                 ),
                 in_=bank[:].rearrange("p (il u q) -> p il q u", il=2, u=2),
             )
 
-        def quantise_w_out(pair, h):
-            rows = slice(256 * pair, 256 * (pair + 1))
+        def quantise_w_out(h):
             nc.vector.quantize_mx(
-                out=wo_codes[:, h, rows].bitcast(FP8X4),
-                scales=wo_scales[:, h, rows],
-                in_=wo_grouped[:, h, 4 * 256 * pair : 4 * 256 * (pair + 1)],
+                out=wo_codes[:, h, :].bitcast(FP8X4), scales=wo_scales[:, h, :], in_=wo_grouped[:, h, :]
             )
 
-        make_gain()
         flip_x()
         flip_w_in(0, (nc.vector.tensor_copy, nc.scalar.copy))
         turn_for_spreading()
@@ -325,8 +321,8 @@ def tile_mamba3core_s_kernel(
         flip_w_in(1, (nc.vector.tensor_copy, nc.scalar.copy))
         token_matmul_slice(0)
         copy_xi(0)
-        spread_b_imag(0)
         b_real_0 = spread_row(spreads, 0, 3)
+        spread_b_imag(0)
         quantise_w_in_slice(1)
         states_vector("r", 0, b_real_0)
         store("r", 0)
@@ -337,41 +333,39 @@ def tile_mamba3core_s_kernel(
         states_vector("r", 1, b_real_1)
         store("r", 1)
         flip_w_in(2, (nc.scalar.copy, nc.scalar.copy))
-        flip_w_in(3, (nc.vector.tensor_copy, nc.vector.tensor_copy))
+        flip_w_in(3, (nc.scalar.copy, nc.scalar.copy))
         store("i", 0)
-        quantise_w_in(1)
-        column_matmul(0)
+        make_gain()
         b_imag_1 = spread_row(spreads, 5, 3)
         states_vector("i", 1, b_imag_1)
         store("i", 1)
-        flip_w_out(0, 0)
-        flip_w_out(1, 0)
-        make_y(0)
+        quantise_w_in(1)
+        column_matmul(0)
+        flip_w_out(0, 0, nc.scalar.copy)
+        flip_w_out(1, 0, nc.scalar.copy)
         token_matmul(1)
         copy_xi(2)
         column_matmul(1)
-        quantise_w_out(0, 0)
-        quantise_w_out(1, 0)
+        make_y(0)
         spread_b_imag(2)
         states_gpsimd("i", 2)
         b_real_2 = spread_row(spreads, 2, 3)
+        quantise_w_out(0)
         make_y(1)
         states_vector("r", 2, b_real_2)
         store("r", 2)
-        flip_w_out(0, 1)
-        flip_w_out(1, 1)
+        flip_w_out(0, 1, nc.scalar.copy)
+        flip_w_out(1, 1, nc.scalar.copy)
         copy_xi(3)
-        quantise_y(0)
-        quantise_y(1)
-        quantise_w_out(0, 1)
-        quantise_w_out(1, 1)
+        quantise_y()
+        quantise_w_out(1)
         spread_b_imag(3)
         states_gpsimd("i", 3)
+        store("i", 2)
         b_real_3 = spread_row(spreads, 3, 3)
         spread_norm_w()
         states_vector("r", 3, b_real_3)
         store("r", 3)
-        store("i", 2)
         store("i", 3)
 
         acc = [xi_col.tile([P, HALF], F32, name="acc", tag="xi_col") for n in range(2)]
@@ -407,10 +401,10 @@ def tile_mamba3core_s_kernel(
             nc.vector.tensor_tensor(out=weighted[:, cols], in0=acc[n][:], in1=norm_w_all[:, cols], op=ALU.mult)
 
         square_half(0)
-        weigh_half(1)
         nc.scalar.activation(out=mean_sq[:], in_=sum_sq[:, 0:1], func=ACT.Identity, bias=eps[:], scale=1.0 / D)
-        square_half(1)
         weigh_half(0)
+        square_half(1)
+        weigh_half(1)
         nc.scalar.activation(
             out=inv_rms[:], in_=sum_sq[:, 1:2], func=ACT.Abs_reciprocal_sqrt, bias=mean_sq[:], scale=1.0 / D
         )

@@ -53,6 +53,8 @@ def tile_mamba3core_s_kernel(
         make_identity(nc, ident[:])
         eps = keep.tile([P, 1], F32)
         nc.vector.memset(eps[:], EPS)
+        zeros = keep.tile([P, 3 * P], F32)
+        nc.vector.memset(zeros[:], 0.0)
 
         x_sb = keep.tile([P, D], BF16)
         nc.sync.dma_start(out=x_sb[:], in_=x_rows)
@@ -314,6 +316,8 @@ def tile_mamba3core_s_kernel(
                 out=wo_codes[:, h, :].bitcast(FP8X4), scales=wo_scales[:, h, :], in_=wo_grouped[:, h, :]
             )
 
+        idle = spreads.tile([P, BANK], F32, name="idle", tag="flip")
+        nc.tensor.matmul(idle[:, 0 : 3 * P], zeros[:, 0:P], zeros[:], start=True, stop=True)
         flip_x()
         flip_w_in(0, (nc.vector.tensor_copy, nc.scalar.copy))
         turn_for_spreading()

@@ -48,13 +48,13 @@ def tile_mamba3core_s_kernel(
         ctx.enter_context(tc.manual_schedule())
 
         vec_rows = keep.tile([P, SLICE_FLAT], BF16)
+        zeros = keep.tile([P, P], F32)
+        nc.vector.memset(zeros[:], 0.0)
         nc.vector.memset(vec_rows[:].bitcast(F32), 0.0)
         ident = keep.tile([P, P], F32)
         make_identity(nc, ident[:])
         eps = keep.tile([P, 1], F32)
         nc.vector.memset(eps[:], EPS)
-        zeros = keep.tile([P, 3 * P], F32)
-        nc.vector.memset(zeros[:], 0.0)
 
         x_sb = keep.tile([P, D], BF16)
         nc.sync.dma_start(out=x_sb[:], in_=x_rows)
@@ -79,24 +79,28 @@ def tile_mamba3core_s_kernel(
         load_w_in(2)
         load_w_in(3)
         wo_sb = keep.tile([P, 4, COLS], BF16)
-        for pair in range(2):
+
+        def load_w_out(pair):
             nc.sync.dma_start(
                 out=wo_sb[:, 2 * pair : 2 * pair + 2, :],
                 in_=W_out[256 * pair : 256 * (pair + 1), :].rearrange("(i q) k -> q i k", q=P),
             )
+
+        load_w_out(0)
         own = keep.tile([P, 4, PASSES, 16], BF16)
         for v, src in enumerate((B_real, B_imag, C_real, C_imag)):
             nc.sync.dma_start(
                 out=own[:, v, :, 0 : 4 * STATES],
                 in_=src.rearrange("h (p t) n -> p h (t n)", t=4),
             )
+        load_w_out(1)
         warm = keep.tile([P, 1], F32)
         nc.scalar.activation(out=warm[:], in_=eps[:], func=ACT.Abs_reciprocal_sqrt)
 
         vec_words = vec_rows[:].bitcast(F32)
         vec_cols = keep.tile([P, 3, 16], F32)
-        rr = keep.tile([P, PASSES, 4 * STATES], F32)
-        ii = keep.tile([P, PASSES, 4 * STATES], F32)
+        cb = keep.tile([P, 2, PASSES, 4 * STATES], F32)
+        terms = keep.tile([P, PASSES, 4 * STATES], F32)
         gain = keep.tile([P, PASSES, 4], F32)
 
         def turn_for_spreading():
@@ -111,13 +115,18 @@ def tile_mamba3core_s_kernel(
 
         def make_gain():
             used = slice(0, 4 * STATES)
-            nc.gpsimd.tensor_tensor(out=rr[:], in0=own[:, 2, :, used], in1=own[:, 0, :, used], op=ALU.mult)
-            nc.gpsimd.tensor_tensor(out=ii[:], in0=own[:, 3, :, used], in1=own[:, 1, :, used], op=ALU.mult)
-            nc.gpsimd.tensor_tensor(out=rr[:], in0=rr[:], in1=ii[:], op=ALU.subtract)
-            terms = rr[:].rearrange("p h (t n) -> p (h t) n", n=STATES)
-            total = gain[:].rearrange("p h t -> p (h t)")
-            nc.gpsimd.tensor_tensor(out=total, in0=terms[:, :, 0], in1=terms[:, :, 1], op=ALU.add)
-            nc.gpsimd.tensor_tensor(out=total, in0=total, in1=terms[:, :, 2], op=ALU.add)
+            nc.gpsimd.tensor_tensor(
+                out=cb[:], in0=own[:, 2:4, :, used], in1=own[:, 0:2, :, used], op=ALU.mult
+            )
+            nc.gpsimd.tensor_tensor(out=terms[:], in0=cb[:, 0, :, :], in1=cb[:, 1, :, :], op=ALU.subtract)
+
+        def sum_gain():
+            nc.vector.tensor_reduce(
+                out=gain[:].rearrange("p h t -> p (h t)"),
+                in_=terms[:].rearrange("p h (t n) -> p (h t) n", n=STATES),
+                axis=mybir.AxisListType.X,
+                op=ALU.add,
+            )
 
         def spread_row(pool, row, slices):
             bank = pool.tile([P, BANK], F32, tag="flip")
@@ -138,6 +147,10 @@ def tile_mamba3core_s_kernel(
                 out=b_imag_all[:].bitcast(F32)[:, SLICE_WORDS * g : SLICE_WORDS * (g + 1)],
                 in_=bank[:, 0:SLICE_WORDS],
             )
+
+        def copy_b_imag(g, bank, words):
+            first = SLICE_WORDS * g
+            nc.scalar.copy(out=b_imag_all[:].bitcast(F32)[:, first : first + words], in_=bank[:, 0:words])
 
         def spread_norm_w():
             bank = spread_row(flips, NORM_ROW, 2)
@@ -256,25 +269,32 @@ def tile_mamba3core_s_kernel(
                 in_=xi_by_token[g],
             )
 
-        def states(which, g, engine, b_all):
-            flat = slice(SLICE_FLAT * g, SLICE_FLAT * (g + 1))
-            cols = slice(HALF * g, HALF * (g + 1))
+        def states(which, g, engine, b_words, part=(0, 1)):
+            width = HALF // part[1]
+            first = HALF * g + width * part[0]
+            flat = slice(STATES * first, STATES * (first + width))
             engine.tensor_tensor(
                 out=state_sb[which][:, flat].rearrange("t (c n) -> t c n", n=STATES),
-                in0=xi_sb[:, cols].unsqueeze(2).to_broadcast([P, HALF, STATES]),
-                in1=b_all.rearrange("t (c n) -> t c n", n=STATES),
+                in0=xi_sb[:, first : first + width].unsqueeze(2).to_broadcast([P, width, STATES]),
+                in1=b_words.bitcast(BF16)[
+                    :, STATES * width * part[0] : STATES * width * (part[0] + 1)
+                ].rearrange("t (c n) -> t c n", n=STATES),
                 op=ALU.mult,
             )
 
-        def store(which, g):
-            flat = slice(SLICE_FLAT * g, SLICE_FLAT * (g + 1))
-            nc.sync.dma_start(out=state_rows[which][:, flat], in_=state_sb[which][:, flat])
+        def store(which, g, part=(0, 1)):
+            width = SLICE_FLAT // part[1]
+            first = SLICE_FLAT * g + width * part[0]
+            nc.sync.dma_start(
+                out=state_rows[which][:, first : first + width], in_=state_sb[which][:, first : first + width]
+            )
 
-        def states_gpsimd(which, g):
-            states(which, g, nc.gpsimd, b_imag_all[:, SLICE_FLAT * g : SLICE_FLAT * (g + 1)])
+        def states_gpsimd(which, g, part=(0, 1)):
+            words = b_imag_all[:].bitcast(F32)[:, SLICE_WORDS * g : SLICE_WORDS * (g + 1)]
+            states(which, g, nc.gpsimd, words, part)
 
-        def states_vector(which, g, bank):
-            states(which, g, nc.vector, bank[:, 0:SLICE_WORDS].bitcast(BF16))
+        def states_vector(which, g, bank, part=(0, 1)):
+            states(which, g, nc.vector, bank[:, 0:SLICE_WORDS], part)
 
         def make_y(h):
             nc.vector.tensor_tensor(
@@ -316,64 +336,10 @@ def tile_mamba3core_s_kernel(
                 out=wo_codes[:, h, :].bitcast(FP8X4), scales=wo_scales[:, h, :], in_=wo_grouped[:, h, :]
             )
 
-        idle = spreads.tile([P, BANK], F32, name="idle", tag="flip")
-        nc.tensor.matmul(idle[:, 0 : 3 * P], zeros[:, 0:P], zeros[:], start=True, stop=True)
-        flip_x()
-        flip_w_in(0, (nc.vector.tensor_copy, nc.scalar.copy))
-        turn_for_spreading()
-        quantise_w_in_slice(0)
-        flip_w_in(1, (nc.vector.tensor_copy, nc.scalar.copy))
-        token_matmul_slice(0)
-        copy_xi(0)
-        b_real_0 = spread_row(spreads, 0, 3)
-        spread_b_imag(0)
-        quantise_w_in_slice(1)
-        states_vector("r", 0, b_real_0)
-        store("r", 0)
-        states_gpsimd("i", 0)
-        token_matmul_slice(1)
-        b_real_1 = spread_row(spreads, 1, 3)
-        copy_xi(1)
-        states_vector("r", 1, b_real_1)
-        store("r", 1)
-        flip_w_in(2, (nc.scalar.copy, nc.scalar.copy))
-        flip_w_in(3, (nc.scalar.copy, nc.scalar.copy))
-        store("i", 0)
-        make_gain()
-        b_imag_1 = spread_row(spreads, 5, 3)
-        states_vector("i", 1, b_imag_1)
-        store("i", 1)
-        quantise_w_in(1)
-        column_matmul(0)
-        flip_w_out(0, 0, nc.scalar.copy)
-        flip_w_out(1, 0, nc.scalar.copy)
-        token_matmul(1)
-        copy_xi(2)
-        column_matmul(1)
-        make_y(0)
-        spread_b_imag(2)
-        states_gpsimd("i", 2)
-        b_real_2 = spread_row(spreads, 2, 3)
-        quantise_w_out(0)
-        make_y(1)
-        states_vector("r", 2, b_real_2)
-        store("r", 2)
-        flip_w_out(0, 1, nc.scalar.copy)
-        flip_w_out(1, 1, nc.scalar.copy)
-        copy_xi(3)
-        quantise_y()
-        quantise_w_out(1)
-        spread_b_imag(3)
-        states_gpsimd("i", 3)
-        store("i", 2)
-        b_real_3 = spread_row(spreads, 3, 3)
-        spread_norm_w()
-        states_vector("r", 3, b_real_3)
-        store("r", 3)
-        store("i", 3)
+        acc = {}
 
-        acc = [xi_col.tile([P, HALF], F32, name="acc", tag="xi_col") for n in range(2)]
-        for n in range(2):
+        def second_matmul(n):
+            acc[n] = xi_col.tile([P, HALF], F32, name="acc", tag="xi_col")
             cols = slice(HALF * n, HALF * (n + 1))
             for h in range(PASSES):
                 nc.tensor.matmul_mx(
@@ -387,33 +353,113 @@ def tile_mamba3core_s_kernel(
                 )
 
         squares = keep.tile([P, D], F32)
-        sum_sq = keep.tile([P, 2], F32)
+        sum_sq = [keep.tile([P, 1], F32, name="sum_sq0"), keep.tile([P, 1], F32, name="sum_sq1")]
         weighted = keep.tile([P, D], F32)
         mean_sq = keep.tile([P, 1], F32)
         inv_rms = keep.tile([P, 1], F32)
+        res = keep.tile([P, D], F32)
 
         def square_half(n):
             nc.scalar.activation(
                 out=squares[:, HALF * n : HALF * (n + 1)],
                 in_=acc[n][:],
                 func=ACT.Square,
-                accum_out=sum_sq[:, n : n + 1],
+                accum_out=sum_sq[n][:],
+            )
+
+        def first_mean():
+            nc.scalar.activation(
+                out=mean_sq[:], in_=sum_sq[0][:], func=ACT.Identity, bias=eps[:], scale=1.0 / D
+            )
+
+        def inverse_root():
+            nc.scalar.activation(
+                out=inv_rms[:], in_=sum_sq[1][:], func=ACT.Abs_reciprocal_sqrt, bias=mean_sq[:], scale=1.0 / D
             )
 
         def weigh_half(n):
             cols = slice(HALF * n, HALF * (n + 1))
             nc.vector.tensor_tensor(out=weighted[:, cols], in0=acc[n][:], in1=norm_w_all[:, cols], op=ALU.mult)
 
+        def finish_half(n):
+            cols = slice(HALF * n, HALF * (n + 1))
+            nc.vector.scalar_tensor_tensor(
+                out=res[:, cols],
+                in0=weighted[:, cols],
+                scalar=inv_rms[:],
+                in1=x_sb[:, cols],
+                op0=ALU.mult,
+                op1=ALU.add,
+            )
+            nc.sync.dma_start(out=res_rows[:, cols], in_=res[:, cols])
+
+        idle = spreads.tile([P, BANK], F32, name="idle", tag="flip")
+        nc.tensor.matmul(idle[:, 0 : 3 * P], zeros[:], zeros[:, 0:1].to_broadcast([P, 3 * P]), start=True, stop=True)
+        flip_x()
+        flip_w_in(0, (nc.vector.tensor_copy, nc.scalar.copy))
+        turn_for_spreading()
+        quantise_w_in_slice(0)
+        flip_w_in(1, (nc.vector.tensor_copy, nc.scalar.copy))
+        b_real_0 = spread_row(spreads, 0, 3)
+        quantise_w_in_slice(1)
+        token_matmul_slice(0)
+        copy_xi(0)
+        flip_w_in(2, (nc.scalar.copy, nc.scalar.copy))
+        b_real_1 = spread_row(spreads, 1, 3)
+        states_vector("r", 0, b_real_0)
+        store("r", 0)
+        flip_w_in(3, (nc.scalar.copy, nc.scalar.copy))
+        token_matmul_slice(1)
+        copy_xi(1)
+        spread_b_imag(0)
+        make_gain()
+        states_gpsimd("i", 0)
+        quantise_w_in(1)
+        states_vector("r", 1, b_real_1)
+        store("r", 1)
+        store("i", 0)
+        flip_w_out(0, 0, nc.scalar.copy)
+        column_matmul(0)
+        token_matmul(1)
+        column_matmul(1)
+        copy_xi(2)
+        sum_gain()
+        make_y(0)
+        make_y(1)
+        b_imag_1 = spread_row(spreads, 5, 3)
+        copy_b_imag(1, b_imag_1, SLICE_WORDS // 2)
+        states_vector("i", 1, b_imag_1, (1, 2))
+        states_gpsimd("i", 1, (0, 2))
+        store("i", 1)
+        spread_b_imag(2)
+        flip_w_out(1, 0, nc.scalar.copy)
+        flip_w_out(0, 1, nc.scalar.copy)
+        copy_xi(3)
+        b_real_2 = spread_row(spreads, 2, 3)
+        states_vector("r", 2, b_real_2)
+        store("r", 2)
+        states_gpsimd("i", 2)
+        flip_w_out(1, 1, nc.scalar.copy)
+        quantise_y()
+        quantise_w_out(0)
+        quantise_w_out(1)
+        b_real_3 = spread_row(spreads, 3, 3)
+        b_imag_3 = spread_row(spreads, 7, 3)
+        copy_b_imag(3, b_imag_3, SLICE_WORDS // 2)
+        states_gpsimd("i", 3, (0, 2))
+        store("i", 2)
+        spread_norm_w()
+        second_matmul(0)
+        second_matmul(1)
+        states_vector("r", 3, b_real_3)
+        store("r", 3)
+        states_vector("i", 3, b_imag_3, (1, 2))
+        store("i", 3)
         square_half(0)
-        nc.scalar.activation(out=mean_sq[:], in_=sum_sq[:, 0:1], func=ACT.Identity, bias=eps[:], scale=1.0 / D)
-        weigh_half(0)
+        first_mean()
         square_half(1)
+        weigh_half(0)
+        inverse_root()
         weigh_half(1)
-        nc.scalar.activation(
-            out=inv_rms[:], in_=sum_sq[:, 1:2], func=ACT.Abs_reciprocal_sqrt, bias=mean_sq[:], scale=1.0 / D
-        )
-        res = keep.tile([P, D], F32)
-        nc.vector.scalar_tensor_tensor(
-            out=res[:], in0=weighted[:], scalar=inv_rms[:], in1=x_sb[:], op0=ALU.mult, op1=ALU.add
-        )
-        nc.sync.dma_start(out=res_rows, in_=res[:])
+        finish_half(0)
+        finish_half(1)

@@ -338,10 +338,11 @@ def tile_mamba3core_s_kernel(
 
         acc = {}
 
-        def second_matmul(n):
-            acc[n] = xi_col.tile([P, HALF], F32, name="acc", tag="xi_col")
-            cols = slice(HALF * n, HALF * (n + 1))
-            for h in range(PASSES):
+        def second_matmul(h):
+            for n in range(2):
+                if h == 0:
+                    acc[n] = xi_col.tile([P, HALF], F32, name="acc", tag="xi_col")
+                cols = slice(HALF * n, HALF * (n + 1))
                 nc.tensor.matmul_mx(
                     out=acc[n][:],
                     lhsT=y_codes[:, h, :].bitcast(FP8X4),
@@ -400,60 +401,58 @@ def tile_mamba3core_s_kernel(
         turn_for_spreading()
         quantise_w_in_slice(0)
         flip_w_in(1, (nc.vector.tensor_copy, nc.scalar.copy))
-        b_real_0 = spread_row(spreads, 0, 3)
         quantise_w_in_slice(1)
+        b_real_0 = spread_row(spreads, 0, 3)
         token_matmul_slice(0)
         copy_xi(0)
-        flip_w_in(2, (nc.scalar.copy, nc.scalar.copy))
-        b_real_1 = spread_row(spreads, 1, 3)
+        flip_w_in(2, (nc.scalar.copy, nc.vector.tensor_copy))
+        flip_w_in(3, (nc.scalar.copy, nc.scalar.copy))
         states_vector("r", 0, b_real_0)
         store("r", 0)
-        flip_w_in(3, (nc.scalar.copy, nc.scalar.copy))
+        b_real_1 = spread_row(spreads, 1, 3)
         token_matmul_slice(1)
         copy_xi(1)
         spread_b_imag(0)
+        quantise_w_in(1)
         make_gain()
         states_gpsimd("i", 0)
-        quantise_w_in(1)
+        column_matmul(0)
         states_vector("r", 1, b_real_1)
         store("r", 1)
         store("i", 0)
-        flip_w_out(0, 0, nc.scalar.copy)
-        column_matmul(0)
-        token_matmul(1)
-        column_matmul(1)
-        copy_xi(2)
-        sum_gain()
-        make_y(0)
-        make_y(1)
         b_imag_1 = spread_row(spreads, 5, 3)
         copy_b_imag(1, b_imag_1, SLICE_WORDS // 2)
+        flip_w_out(0, 0, nc.scalar.copy)
+        token_matmul(1)
+        copy_xi(2)
+        column_matmul(1)
+        flip_w_out(1, 0, nc.scalar.copy)
+        sum_gain()
+        make_y(0)
         states_vector("i", 1, b_imag_1, (1, 2))
         states_gpsimd("i", 1, (0, 2))
         store("i", 1)
-        spread_b_imag(2)
-        flip_w_out(1, 0, nc.scalar.copy)
-        flip_w_out(0, 1, nc.scalar.copy)
-        copy_xi(3)
+        make_y(1)
+        quantise_y()
         b_real_2 = spread_row(spreads, 2, 3)
         states_vector("r", 2, b_real_2)
         store("r", 2)
+        spread_b_imag(2)
         states_gpsimd("i", 2)
-        flip_w_out(1, 1, nc.scalar.copy)
-        quantise_y()
-        quantise_w_out(0)
-        quantise_w_out(1)
-        b_real_3 = spread_row(spreads, 3, 3)
-        b_imag_3 = spread_row(spreads, 7, 3)
-        copy_b_imag(3, b_imag_3, SLICE_WORDS // 2)
-        states_gpsimd("i", 3, (0, 2))
         store("i", 2)
+        flip_w_out(0, 1, nc.scalar.copy)
+        flip_w_out(1, 1, nc.scalar.copy)
+        copy_xi(3)
+        quantise_w_out(0)
+        b_real_3 = spread_row(spreads, 3, 3)
+        spread_b_imag(3)
+        states_gpsimd("i", 3)
+        quantise_w_out(1)
         spread_norm_w()
         second_matmul(0)
         second_matmul(1)
         states_vector("r", 3, b_real_3)
         store("r", 3)
-        states_vector("i", 3, b_imag_3, (1, 2))
         store("i", 3)
         square_half(0)
         first_mean()

@@ -396,6 +396,7 @@ def tile_mamba3core_s_kernel(
 
         idle = spreads.tile([P, BANK], F32, name="idle", tag="flip")
         nc.tensor.matmul(idle[:, 0 : 3 * P], zeros[:], zeros[:, 0:1].to_broadcast([P, 3 * P]), start=True, stop=True)
+        make_gain()
         flip_x()
         flip_w_in(0, (nc.vector.tensor_copy, nc.scalar.copy))
         turn_for_spreading()
@@ -409,54 +410,53 @@ def tile_mamba3core_s_kernel(
         flip_w_in(3, (nc.scalar.copy, nc.scalar.copy))
         states_vector("r", 0, b_real_0)
         store("r", 0)
+        quantise_w_in(1)
         b_real_1 = spread_row(spreads, 1, 3)
         token_matmul_slice(1)
         copy_xi(1)
         spread_b_imag(0)
-        quantise_w_in(1)
-        make_gain()
         states_gpsimd("i", 0)
         column_matmul(0)
         states_vector("r", 1, b_real_1)
         store("r", 1)
         store("i", 0)
-        b_imag_1 = spread_row(spreads, 5, 3)
-        copy_b_imag(1, b_imag_1, SLICE_WORDS // 2)
+        spread_b_imag(2)
         flip_w_out(0, 0, nc.scalar.copy)
         token_matmul(1)
         copy_xi(2)
-        column_matmul(1)
-        flip_w_out(1, 0, nc.scalar.copy)
+        states_gpsimd("i", 2)
         sum_gain()
         make_y(0)
-        states_vector("i", 1, b_imag_1, (1, 2))
-        states_gpsimd("i", 1, (0, 2))
+        b_imag_1 = spread_row(spreads, 5, 3)
+        states_vector("i", 1, b_imag_1)
         store("i", 1)
+        column_matmul(1)
+        flip_w_out(1, 0, nc.scalar.copy)
+        flip_w_out(0, 1, nc.scalar.copy)
+        copy_xi(3)
         make_y(1)
-        quantise_y()
         b_real_2 = spread_row(spreads, 2, 3)
         states_vector("r", 2, b_real_2)
-        store("r", 2)
-        spread_b_imag(2)
-        states_gpsimd("i", 2)
         store("i", 2)
-        flip_w_out(0, 1, nc.scalar.copy)
+        store("r", 2)
         flip_w_out(1, 1, nc.scalar.copy)
-        copy_xi(3)
-        quantise_w_out(0)
         b_real_3 = spread_row(spreads, 3, 3)
-        spread_b_imag(3)
-        states_gpsimd("i", 3)
+        quantise_w_out(0)
+        quantise_y()
         quantise_w_out(1)
         spread_norm_w()
         second_matmul(0)
+        b_imag_3 = spread_row(spreads, 7, 3)
+        copy_b_imag(3, b_imag_3, SLICE_WORDS // 2)
         second_matmul(1)
         states_vector("r", 3, b_real_3)
         store("r", 3)
+        states_vector("i", 3, b_imag_3, (1, 2))
+        states_gpsimd("i", 3, (0, 2))
         store("i", 3)
         square_half(0)
-        first_mean()
         square_half(1)
+        first_mean()
         weigh_half(0)
         inverse_root()
         weigh_half(1)

@@ -241,16 +241,21 @@ def tile_mamba3core_s_kernel(
                 token_pass(bank[:, 64 * t : 64 * (t + 1)], slice(first, first + 64))
             xi_by_token[g] = bank[:, 0:HALF].rearrange("x (t p) -> x p t", t=4)
 
-        def token_matmul(h):
+        def token_matmul(h, halves=(0, 1)):
             bank = xi_tok.tile([P, D], F32, name="xi_by_token", tag="xi_tok")
             token_pass(bank[:], slice(D * h, D * (h + 1)))
-            for half in range(2):
+            for half in halves:
                 xi_by_token[2 * h + half] = bank[:].rearrange("x (t p) -> x p t", t=4)[
                     :, 64 * half : 64 * (half + 1), :
                 ]
 
-        def column_matmul(h):
+        def column_bank(h):
             xi_by_column[h] = xi_col.tile([P, 4, P], F32, name="xi_by_column", tag="xi_col")
+            return xi_by_column[h][:].rearrange("p t x -> p (t x)")
+
+        def column_matmul(h):
+            if h not in xi_by_column:
+                column_bank(h)
             for t in range(4):
                 part = slice(D * h + P * t, D * h + P * (t + 1))
                 nc.tensor.matmul_mx(
@@ -338,13 +343,17 @@ def tile_mamba3core_s_kernel(
 
         acc = {}
 
+        def acc_bank(n):
+            acc[n] = xi_col.tile([P, D], F32, name="acc", tag="xi_col")
+            return acc[n][:]
+
         def second_matmul(h):
             for n in range(2):
-                if h == 0:
-                    acc[n] = xi_col.tile([P, HALF], F32, name="acc", tag="xi_col")
+                if n not in acc:
+                    acc_bank(n)
                 cols = slice(HALF * n, HALF * (n + 1))
                 nc.tensor.matmul_mx(
-                    out=acc[n][:],
+                    out=acc[n][:, 0:HALF],
                     lhsT=y_codes[:, h, :].bitcast(FP8X4),
                     lhsT_scale=y_scales[:, h, :],
                     rhs=wo_codes[:, h, cols].bitcast(FP8X4),
@@ -363,7 +372,7 @@ def tile_mamba3core_s_kernel(
         def square_half(n):
             nc.scalar.activation(
                 out=squares[:, HALF * n : HALF * (n + 1)],
-                in_=acc[n][:],
+                in_=acc[n][:, 0:HALF],
                 func=ACT.Square,
                 accum_out=sum_sq[n][:],
             )
@@ -380,7 +389,7 @@ def tile_mamba3core_s_kernel(
 
         def weigh_half(n):
             cols = slice(HALF * n, HALF * (n + 1))
-            nc.vector.tensor_tensor(out=weighted[:, cols], in0=acc[n][:], in1=norm_w_all[:, cols], op=ALU.mult)
+            nc.vector.tensor_tensor(out=weighted[:, cols], in0=acc[n][:, 0:HALF], in1=norm_w_all[:, cols], op=ALU.mult)
 
         def finish_half(n):
             cols = slice(HALF * n, HALF * (n + 1))
@@ -394,8 +403,28 @@ def tile_mamba3core_s_kernel(
             )
             nc.sync.dma_start(out=res_rows[:, cols], in_=res[:, cols])
 
-        idle = spreads.tile([P, BANK], F32, name="idle", tag="flip")
-        nc.tensor.matmul(idle[:, 0 : 3 * P], zeros[:], zeros[:, 0:1].to_broadcast([P, 3 * P]), start=True, stop=True)
+        idle_bank = spreads.tile([P, BANK], F32, name="idle_bank", tag="flip")
+
+        def idle_zeros(width):
+            nc.tensor.matmul(
+                idle_bank[:, 0:width], zeros[:], zeros[:, 0:1].to_broadcast([P, width]), start=True, stop=True
+            )
+
+        def idle_x():
+            nc.tensor.matmul_mx(
+                out=idle_bank[:, 0:P],
+                lhsT=x_codes[:].bitcast(FP8X4),
+                lhsT_scale=x_scales[:],
+                rhs=x_codes[:].bitcast(FP8X4),
+                rhs_scale=x_scales[:],
+                start=True,
+                stop=True,
+            )
+
+        def idle_pass(bank):
+            token_pass(bank, slice(0, D))
+
+        idle_zeros(3 * P)
         make_gain()
         flip_x()
         flip_w_in(0, (nc.vector.tensor_copy, nc.scalar.copy))
@@ -412,7 +441,7 @@ def tile_mamba3core_s_kernel(
         store("r", 0)
         quantise_w_in(1)
         b_real_1 = spread_row(spreads, 1, 3)
-        token_matmul_slice(1)
+        token_matmul(0, (1,))
         copy_xi(1)
         spread_b_imag(0)
         states_gpsimd("i", 0)
@@ -421,13 +450,14 @@ def tile_mamba3core_s_kernel(
         store("r", 1)
         store("i", 0)
         spread_b_imag(2)
+        b_imag_1 = spread_row(spreads, 5, 3)
         flip_w_out(0, 0, nc.scalar.copy)
+        idle_pass(column_bank(1))
         token_matmul(1)
         copy_xi(2)
         states_gpsimd("i", 2)
         sum_gain()
         make_y(0)
-        b_imag_1 = spread_row(spreads, 5, 3)
         states_vector("i", 1, b_imag_1)
         store("i", 1)
         column_matmul(1)
@@ -445,6 +475,10 @@ def tile_mamba3core_s_kernel(
         quantise_y()
         quantise_w_out(1)
         spread_norm_w()
+        idle_pass(acc_bank(0))
+        idle_pass(acc[0][:])
+        idle_pass(acc[0][:])
+        idle_pass(acc[0][:])
         second_matmul(0)
         b_imag_3 = spread_row(spreads, 7, 3)
         copy_b_imag(3, b_imag_3, SLICE_WORDS // 2)

from contextlib import ExitStack

from concourse import mybir
from concourse.masks import make_identity

F32 = mybir.dt.float32
BF16 = mybir.dt.bfloat16
U32 = mybir.dt.uint32
U8 = mybir.dt.uint8
FP8X4 = mybir.dt.float8_e4m3fn_x4
ALU = mybir.AluOpType
ACT = mybir.ActivationFunctionType

P = 128
D = 512
PASSES = 2
STATES = 3
COLS = PASSES * D
HALF = 256
SLICE_FLAT = HALF * STATES
SLICE_WORDS = SLICE_FLAT // 2
SLICES = COLS // HALF
FLAT = SLICES * SLICE_FLAT
BANK = 512
NORM_ROW = 2 * SLICES
EPS = 2.0 ** -23

FLOPS = 2 * (2 * P * D * COLS)


def tile_mamba3core_s_kernel(
    tc, x, W_in, W_out, A_theta, B_real, B_imag, C_real, C_imag, norm_w, out_0, out_1, out_2
):
    nc = tc.nc
    x_rows = x.flatten_outer_dims()
    res_rows = out_0.flatten_outer_dims()
    state_rows = {
        "r": out_1.rearrange("b l c d n -> (b l) (c d n)"),
        "i": out_2.rearrange("b l c d n -> (b l) (c d n)"),
    }

    with ExitStack() as ctx:
        keep = ctx.enter_context(tc.tile_pool(name="keep", bufs=1))
        flips = ctx.enter_context(tc.psum_pool(name="flips", bufs=3))
        spreads = ctx.enter_context(tc.psum_pool(name="spreads", bufs=2))
        xi_tok = ctx.enter_context(tc.psum_pool(name="xi_tok", bufs=1))
        xi_col = ctx.enter_context(tc.psum_pool(name="xi_col", bufs=2))
        ctx.enter_context(tc.manual_schedule())

        vec_rows = keep.tile([P, SLICE_FLAT], BF16)
        zeros = keep.tile([P, P], F32)
        nc.vector.memset(zeros[:], 0.0)
        nc.vector.memset(vec_rows[:].bitcast(F32), 0.0)
        ident = keep.tile([P, P], F32)
        make_identity(nc, ident[:])
        eps = keep.tile([P, 1], F32)
        nc.vector.memset(eps[:], EPS)

        x_sb = keep.tile([P, D], BF16)
        nc.sync.dma_start(out=x_sb[:], in_=x_rows)
        wi_sb = keep.tile([P, SLICES, 2 * D], BF16)

        def load_w_in(g):
            nc.sync.dma_start(
                out=wi_sb[:, g, :],
                in_=W_in[HALF * g : HALF * (g + 1), :].rearrange("(q e) k -> q (e k)", e=2),
            )

        load_w_in(0)
        for v, src in enumerate((B_real, B_imag)):
            nc.sync.dma_start(
                out=vec_rows[SLICES * v : SLICES * (v + 1), :],
                in_=src.rearrange("a d n -> (a d n)").rearrange("(g f) -> g f", f=SLICE_FLAT),
            )
        nc.sync.dma_start(
            out=vec_rows[NORM_ROW : NORM_ROW + 1, 0:D], in_=norm_w.rearrange("(o d) -> o d", o=1)
        )
        load_w_in(1)
        load_w_in(2)
        load_w_in(3)
        wo_sb = keep.tile([P, 4, COLS], BF16)

        def load_w_out(pair):
            nc.sync.dma_start(
                out=wo_sb[:, 2 * pair : 2 * pair + 2, :],
                in_=W_out[256 * pair : 256 * (pair + 1), :].rearrange("(i q) k -> q i k", q=P),
            )

        load_w_out(0)
        own = keep.tile([P, 4, PASSES, 16], BF16)
        for v, src in enumerate((B_real, B_imag, C_real, C_imag)):
            nc.sync.dma_start(
                out=own[:, v, :, 0 : 4 * STATES],
                in_=src.rearrange("h (p t) n -> p h (t n)", t=4),
            )
        load_w_out(1)
        warm = keep.tile([P, 1], F32)
        nc.scalar.activation(out=warm[:], in_=eps[:], func=ACT.Abs_reciprocal_sqrt)

        vec_words = vec_rows[:].bitcast(F32)
        vec_cols = keep.tile([P, 3, 16], F32)
        cb = keep.tile([P, 2, PASSES, 4 * STATES], F32)
        terms = keep.tile([P, PASSES, 4 * STATES], F32)
        gain = keep.tile([P, PASSES, 4], F32)

        def turn_for_spreading():
            bank = flips.tile([P, BANK], F32, tag="flip")
            for s in range(3):
                nc.tensor.transpose(
                    bank[:, P * s : P * (s + 1)], vec_words[:, P * s : P * (s + 1)], ident[:]
                )
            nc.scalar.copy(
                out=vec_cols[:], in_=bank[:, 0 : 3 * P].rearrange("w (s r) -> w s r", s=3)[:, :, 0:16]
            )

        def make_gain():
            used = slice(0, 4 * STATES)
            nc.gpsimd.tensor_tensor(
                out=cb[:], in0=own[:, 2:4, :, used], in1=own[:, 0:2, :, used], op=ALU.mult
            )
            nc.gpsimd.tensor_tensor(out=terms[:], in0=cb[:, 0, :, :], in1=cb[:, 1, :, :], op=ALU.subtract)

        def sum_gain():
            nc.vector.tensor_reduce(
                out=gain[:].rearrange("p h t -> p (h t)"),
                in_=terms[:].rearrange("p h (t n) -> p (h t) n", n=STATES),
                axis=mybir.AxisListType.X,
                op=ALU.add,
            )

        def spread_row(pool, row, slices):
            bank = pool.tile([P, BANK], F32, tag="flip")
            for s in range(slices):
                nc.tensor.transpose(
                    bank[:, P * s : P * (s + 1)],
                    vec_cols[:, s, row : row + 1].to_broadcast([P, P]),
                    ident[:],
                )
            return bank

        b_imag_all = keep.tile([P, FLAT], BF16)
        norm_w_all = keep.tile([P, D], BF16)

        def spread_b_imag(g):
            bank = spread_row(flips, SLICES + g, 3)
            nc.scalar.copy(
                out=b_imag_all[:].bitcast(F32)[:, SLICE_WORDS * g : SLICE_WORDS * (g + 1)],
                in_=bank[:, 0:SLICE_WORDS],
            )

        def copy_b_imag(g, bank, words):
            first = SLICE_WORDS * g
            nc.scalar.copy(out=b_imag_all[:].bitcast(F32)[:, first : first + words], in_=bank[:, 0:words])

        def spread_norm_w():
            bank = spread_row(flips, NORM_ROW, 2)
            nc.scalar.copy(out=norm_w_all[:].bitcast(F32), in_=bank[:, 0 : D // 2])

        x_grouped = keep.tile([P, P * 4], BF16, align_bytes=64)
        x_codes = keep.tile([P, P], U32, align_bytes=64)
        x_scales = keep.tile([P, P], U8, align_bytes=64)

        def flip_x():
            bank = flips.tile([P, BANK], F32, tag="flip")
            for u in range(2):
                nc.tensor.transpose(
                    bank[:, P * u : P * (u + 1)], x_sb[:].bitcast(F32)[:, u : 2 * P : 2], ident[:]
                )
            nc.vector.tensor_copy(
                out=x_grouped[:].bitcast(F32).rearrange("w (t u) -> w t u", u=2),
                in_=bank[:, 0 : 2 * P].rearrange("w (u t) -> w t u", u=2),
            )
            nc.vector.quantize_mx(out=x_codes[:].bitcast(FP8X4), scales=x_scales[:], in_=x_grouped[:])

        wi_grouped = keep.tile([P, COLS * 4], BF16, align_bytes=64)
        wi_codes = keep.tile([P, COLS], U32, align_bytes=64)
        wi_scales = keep.tile([P, COLS], U8, align_bytes=64)
        wi_words = wi_grouped[:].bitcast(F32).rearrange("w (h r e p u) -> w h r e p u", h=2, r=2, e=2, u=2)

        def flip_w_in(g, copies):
            h, half = divmod(g, 2)
            banks = [flips.tile([P, BANK], F32, name="bank", tag="flip")]
            banks.append(banks[0] if copies[0] == copies[1] else flips.tile([P, BANK], F32, name="bank", tag="flip"))
            for e in range(2):
                for u in range(2):
                    nc.tensor.transpose(
                        banks[e][:, P * (2 * e + u) : P * (2 * e + u + 1)],
                        wi_sb[:, g, :].bitcast(F32)[:, 256 * e + u : 256 * (e + 1) : 2],
                        ident[:],
                    )
            for e in range(2):
                copies[e](
                    out=wi_words[:, h, :, e, 64 * half : 64 * (half + 1), :],
                    in_=banks[e][:, HALF * e : HALF * (e + 1)].rearrange("w (u p r) -> w r p u", u=2, r=2),
                )

        def quantise_w_in_slice(g):
            h, half = divmod(g, 2)
            for t in range(4):
                first = D * h + P * t + 64 * half
                nc.vector.quantize_mx(
                    out=wi_codes[:, first : first + 64].bitcast(FP8X4),
                    scales=wi_scales[:, first : first + 64],
                    in_=wi_grouped[:, 4 * first : 4 * (first + 64)],
                )

        def quantise_w_in(h):
            nc.vector.quantize_mx(
                out=wi_codes[:, D * h : D * (h + 1)].bitcast(FP8X4),
                scales=wi_scales[:, D * h : D * (h + 1)],
                in_=wi_grouped[:, 4 * D * h : 4 * D * (h + 1)],
            )

        state_sb = {
            "r": keep.tile([P, FLAT], F32, name="state_r"),
            "i": keep.tile([P, FLAT], F32, name="state_i"),
        }
        xi_sb = keep.tile([P, COLS], F32)
        y_grouped = keep.tile([P, PASSES, P, 4], BF16, align_bytes=64)
        y_codes = keep.tile([P, PASSES, P], U32, align_bytes=64)
        y_scales = keep.tile([P, PASSES, P], U8, align_bytes=64)
        xi_by_token = {}
        xi_by_column = {}

        def token_pass(out, cols):
            nc.tensor.matmul_mx(
                out=out,
                lhsT=x_codes[:].bitcast(FP8X4),
                lhsT_scale=x_scales[:],
                rhs=wi_codes[:, cols].bitcast(FP8X4),
                rhs_scale=wi_scales[:, cols],
                start=True,
                stop=True,
            )

        def token_matmul_slice(g):
            h, half = divmod(g, 2)
            bank = xi_tok.tile([P, D], F32, name="xi_by_token", tag="xi_tok")
            for t in range(4):
                first = D * h + P * t + 64 * half
                token_pass(bank[:, 64 * t : 64 * (t + 1)], slice(first, first + 64))
            xi_by_token[g] = bank[:, 0:HALF].rearrange("x (t p) -> x p t", t=4)

        def token_matmul(h, halves=(0, 1)):
            bank = xi_tok.tile([P, D], F32, name="xi_by_token", tag="xi_tok")
            token_pass(bank[:], slice(D * h, D * (h + 1)))
            for half in halves:
                xi_by_token[2 * h + half] = bank[:].rearrange("x (t p) -> x p t", t=4)[
                    :, 64 * half : 64 * (half + 1), :
                ]

        def column_bank(h):
            xi_by_column[h] = xi_col.tile([P, 4, P], F32, name="xi_by_column", tag="xi_col")
            return xi_by_column[h][:].rearrange("p t x -> p (t x)")

        def column_matmul(h):
            if h not in xi_by_column:
                column_bank(h)
            for t in range(4):
                part = slice(D * h + P * t, D * h + P * (t + 1))
                nc.tensor.matmul_mx(
                    out=xi_by_column[h][:, t, :],
                    lhsT=wi_codes[:, part].bitcast(FP8X4),
                    lhsT_scale=wi_scales[:, part],
                    rhs=x_codes[:].bitcast(FP8X4),
                    rhs_scale=x_scales[:],
                    start=True,
                    stop=True,
                )

        def copy_xi(g):
            nc.scalar.copy(
                out=xi_sb[:, HALF * g : HALF * (g + 1)].rearrange("x (p t) -> x p t", t=4),
                in_=xi_by_token[g],
            )

        def states(which, g, engine, b_words, part=(0, 1)):
            width = HALF // part[1]
            first = HALF * g + width * part[0]
            flat = slice(STATES * first, STATES * (first + width))
            engine.tensor_tensor(
                out=state_sb[which][:, flat].rearrange("t (c n) -> t c n", n=STATES),
                in0=xi_sb[:, first : first + width].unsqueeze(2).to_broadcast([P, width, STATES]),
                in1=b_words.bitcast(BF16)[
                    :, STATES * width * part[0] : STATES * width * (part[0] + 1)
                ].rearrange("t (c n) -> t c n", n=STATES),
                op=ALU.mult,
            )

        def store(which, g, part=(0, 1)):
            width = SLICE_FLAT // part[1]
            first = SLICE_FLAT * g + width * part[0]
            nc.sync.dma_start(
                out=state_rows[which][:, first : first + width], in_=state_sb[which][:, first : first + width]
            )

        def states_gpsimd(which, g, part=(0, 1)):
            words = b_imag_all[:].bitcast(F32)[:, SLICE_WORDS * g : SLICE_WORDS * (g + 1)]
            states(which, g, nc.gpsimd, words, part)

        def states_vector(which, g, bank, part=(0, 1)):
            states(which, g, nc.vector, bank[:, 0:SLICE_WORDS], part)

        def make_y(h):
            nc.vector.tensor_tensor(
                out=y_grouped[:, h, :, :],
                in0=xi_by_column[h][:].rearrange("p j t -> p t j"),
                in1=gain[:, h, :].unsqueeze(1).to_broadcast([P, P, 4]),
                op=ALU.mult,
            )

        def quantise_y():
            nc.vector.quantize_mx(
                out=y_codes[:].rearrange("p h t -> p (h t)").bitcast(FP8X4),
                scales=y_scales[:].rearrange("p h t -> p (h t)"),
                in_=y_grouped[:].rearrange("p h t j -> p (h t j)"),
            )

        wo_grouped = keep.tile([P, PASSES, D * 4], BF16, align_bytes=64)
        wo_codes = keep.tile([P, PASSES, D], U32, align_bytes=64)
        wo_scales = keep.tile([P, PASSES, D], U8, align_bytes=64)

        def flip_w_out(pair, h, copy):
            bank = flips.tile([P, BANK], F32, tag="flip")
            for il in range(2):
                for u in range(2):
                    nc.tensor.transpose(
                        bank[:, P * (2 * il + u) : P * (2 * il + u + 1)],
                        wo_sb[:, 2 * pair + il, :].bitcast(F32)[:, 256 * h + u : 256 * (h + 1) : 2],
                        ident[:],
                    )
            copy(
                out=wo_grouped[:, h, :].bitcast(F32)[:, BANK * pair : BANK * (pair + 1)].rearrange(
                    "p (il q u) -> p il q u", il=2, u=2
                ),
                in_=bank[:].rearrange("p (il u q) -> p il q u", il=2, u=2),
            )

        def quantise_w_out(h):
            nc.vector.quantize_mx(
                out=wo_codes[:, h, :].bitcast(FP8X4), scales=wo_scales[:, h, :], in_=wo_grouped[:, h, :]
            )

        acc = {}

        def acc_bank(n):
            acc[n] = xi_col.tile([P, D], F32, name="acc", tag="xi_col")
            return acc[n][:]

        def second_matmul(h):
            for n in range(2):
                if n not in acc:
                    acc_bank(n)
                cols = slice(HALF * n, HALF * (n + 1))
                nc.tensor.matmul_mx(
                    out=acc[n][:, 0:HALF],
                    lhsT=y_codes[:, h, :].bitcast(FP8X4),
                    lhsT_scale=y_scales[:, h, :],
                    rhs=wo_codes[:, h, cols].bitcast(FP8X4),
                    rhs_scale=wo_scales[:, h, cols],
                    start=(h == 0),
                    stop=(h == PASSES - 1),
                )

        squares = keep.tile([P, D], F32)
        sum_sq = [keep.tile([P, 1], F32, name="sum_sq0"), keep.tile([P, 1], F32, name="sum_sq1")]
        weighted = keep.tile([P, D], F32)
        mean_sq = keep.tile([P, 1], F32)
        inv_rms = keep.tile([P, 1], F32)
        res = keep.tile([P, D], F32)

        def square_half(n):
            nc.scalar.activation(
                out=squares[:, HALF * n : HALF * (n + 1)],
                in_=acc[n][:, 0:HALF],
                func=ACT.Square,
                accum_out=sum_sq[n][:],
            )

        def first_mean():
            nc.scalar.activation(
                out=mean_sq[:], in_=sum_sq[0][:], func=ACT.Identity, bias=eps[:], scale=1.0 / D
            )

        def inverse_root():
            nc.scalar.activation(
                out=inv_rms[:], in_=sum_sq[1][:], func=ACT.Abs_reciprocal_sqrt, bias=mean_sq[:], scale=1.0 / D
            )

        def weigh_half(n):
            cols = slice(HALF * n, HALF * (n + 1))
            nc.vector.tensor_tensor(out=weighted[:, cols], in0=acc[n][:, 0:HALF], in1=norm_w_all[:, cols], op=ALU.mult)

        def finish_half(n):
            cols = slice(HALF * n, HALF * (n + 1))
            nc.vector.scalar_tensor_tensor(
                out=res[:, cols],
                in0=weighted[:, cols],
                scalar=inv_rms[:],
                in1=x_sb[:, cols],
                op0=ALU.mult,
                op1=ALU.add,
            )
            nc.sync.dma_start(out=res_rows[:, cols], in_=res[:, cols])

        idle_bank = spreads.tile([P, BANK], F32, name="idle_bank", tag="flip")

        def idle_zeros(width):
            nc.tensor.matmul(
                idle_bank[:, 0:width], zeros[:], zeros[:, 0:1].to_broadcast([P, width]), start=True, stop=True
            )

        def idle_x():
            nc.tensor.matmul_mx(
                out=idle_bank[:, 0:P],
                lhsT=x_codes[:].bitcast(FP8X4),
                lhsT_scale=x_scales[:],
                rhs=x_codes[:].bitcast(FP8X4),
                rhs_scale=x_scales[:],
                start=True,
                stop=True,
            )

        def idle_pass(bank):
            token_pass(bank, slice(0, D))

        idle_zeros(3 * P)
        make_gain()
        flip_x()
        flip_w_in(0, (nc.vector.tensor_copy, nc.scalar.copy))
        turn_for_spreading()
        quantise_w_in_slice(0)
        flip_w_in(1, (nc.vector.tensor_copy, nc.scalar.copy))
        quantise_w_in_slice(1)
        b_real_0 = spread_row(spreads, 0, 3)
        token_matmul_slice(0)
        copy_xi(0)
        flip_w_in(2, (nc.scalar.copy, nc.vector.tensor_copy))
        flip_w_in(3, (nc.scalar.copy, nc.scalar.copy))
        states_vector("r", 0, b_real_0)
        store("r", 0)
        quantise_w_in(1)
        b_real_1 = spread_row(spreads, 1, 3)
        token_matmul(0, (1,))
        copy_xi(1)
        spread_b_imag(0)
        states_gpsimd("i", 0)
        column_matmul(0)
        states_vector("r", 1, b_real_1)
        store("r", 1)
        store("i", 0)
        spread_b_imag(2)
        b_imag_1 = spread_row(spreads, 5, 3)
        flip_w_out(0, 0, nc.scalar.copy)
        idle_pass(column_bank(1))
        token_matmul(1)
        copy_xi(2)
        states_gpsimd("i", 2)
        sum_gain()
        make_y(0)
        states_vector("i", 1, b_imag_1)
        store("i", 1)
        column_matmul(1)
        flip_w_out(1, 0, nc.scalar.copy)
        flip_w_out(0, 1, nc.scalar.copy)
        copy_xi(3)
        make_y(1)
        b_real_2 = spread_row(spreads, 2, 3)
        states_vector("r", 2, b_real_2)
        store("i", 2)
        store("r", 2)
        flip_w_out(1, 1, nc.scalar.copy)
        b_real_3 = spread_row(spreads, 3, 3)
        quantise_w_out(0)
        quantise_y()
        quantise_w_out(1)
        spread_norm_w()
        idle_pass(acc_bank(0))
        idle_pass(acc[0][:])
        idle_pass(acc[0][:])
        idle_pass(acc[0][:])
        second_matmul(0)
        b_imag_3 = spread_row(spreads, 7, 3)
        copy_b_imag(3, b_imag_3, SLICE_WORDS // 2)
        second_matmul(1)
        states_vector("r", 3, b_real_3)
        store("r", 3)
        states_vector("i", 3, b_imag_3, (1, 2))
        states_gpsimd("i", 3, (0, 2))
        store("i", 3)
        square_half(0)
        square_half(1)
        first_mean()
        weigh_half(0)
        inverse_root()
        weigh_half(1)
        finish_half(0)
        finish_half(1)
